import numpy as np
import ml_dtypes


def mxq(x, axis, fmt="e4m3"):
    dtype, down = {"e4m3": (ml_dtypes.float8_e4m3fn, 7), "e5m2": (ml_dtypes.float8_e5m2, 14)}[fmt]
    v = np.moveaxis(np.asarray(x, np.float32).astype(ml_dtypes.bfloat16).astype(np.float64), axis, -1)
    blocks = v.reshape(v.shape[:-1] + (-1, 32))
    amax = np.abs(blocks).max(-1, keepdims=True)
    byte = np.maximum(np.where(amax > 0, np.frexp(amax)[1] - 1 + 127, 0) - down, 1)
    scale = np.exp2(byte - 127.0)
    codes = (blocks / scale).astype(np.float32).astype(dtype).astype(np.float64)
    return np.moveaxis((codes * scale).reshape(v.shape), -1, axis)


WIDE = False


def mx_kscale(k):
    if not WIDE:
        return np.ones(k)
    levels = np.array([10, -10, 5, -5, 0])
    a = np.random.permutation(np.resize(levels, k // 512 * 4)).reshape(k // 512, 4)
    idx = np.arange(k)
    return np.exp2(a[idx // 512, idx % 128 // 32])


BF16 = ml_dtypes.bfloat16


def bf(x):
    return np.asarray(x, np.float32).astype(BF16)


def f64(x):
    return np.asarray(x).astype(np.float64)


B, H, S, D, N, G = 2, 2, 2048, 512, 256, 1


def setup_inputs():
    s = mx_kscale(D)
    return {"x1": bf(np.random.standard_normal((B, H, S, D)) * s),
            "x2": bf(np.random.standard_normal((B, H, D, N)) / np.sqrt(D) / s[:, None]),
            "clip_val1": bf(2.0 + 0.1 * np.random.standard_normal(G)),
            "clip_val2": bf(2.0 + 0.1 * np.random.standard_normal(G))}


def reference(x1, x2, clip_val1, clip_val2):
    return mxq(f64(x1), 3, "e4m3") @ mxq(f64(x2), 2, "e4m3")

@@ -1,0 +1,193 @@
+from contextlib import ExitStack
+
+import concourse.mybir as mybir
+from concourse.masks import make_identity
+
+FP8X4 = mybir.dt.float8_e4m3fn_x4
+BF16 = mybir.dt.bfloat16
+F32 = mybir.dt.float32
+U32 = mybir.dt.uint32
+U8 = mybir.dt.uint8
+
+P = 128
+HEADS = 4
+ROWS = 2048
+K = 512
+N = 256
+T_HEAD = ROWS // P
+UNIT = 4
+UNITS_HEAD = T_HEAD // UNIT
+NU = HEADS * UNITS_HEAD
+
+FLOPS = 2 * HEADS * ROWS * K * N
+
+PINNED = True
+
+LOADS = [
+    ("x1", 0, 1), ("x2", 0, 0), ("x1", 1, 1), ("x1", 2, 2),
+    ("x2", 1, 0), ("x1", 4, 2), ("x1", 6, 2),
+    ("x2", 2, 0), ("x1", 8, 2), ("x1", 10, 2),
+    ("x2", 3, 0), ("x1", 12, 2), ("x1", 14, 2),
+]
+STORES = [(0, 4), (4, 4), (8, 4), (12, 2), (14, 1), (15, 1)]
+VEC_OUT = (1, 5, 9, 13)
+
+
+def tile_matmul_t_kernel(tc, x1, x2, clip_val1, clip_val2, out):
+    nc = tc.nc
+    x1h = [x1[b, h].rearrange("(p t) k -> p t k", t=T_HEAD) for b in range(2) for h in range(2)]
+    x2h = [x2[b, h].rearrange("(u q e) c -> q u (e c)", u=2, e=2) for b in range(2) for h in range(2)]
+    outh = [out[b, h].rearrange("(p t) n -> p t n", t=T_HEAD) for b in range(2) for h in range(2)]
+
+    with ExitStack() as ctx:
+        keep = ctx.enter_context(tc.tile_pool(name="keep", bufs=1))
+        gpool = ctx.enter_context(tc.tile_pool(name="gpool", bufs=3))
+        cpool = ctx.enter_context(tc.tile_pool(name="cpool", bufs=3))
+        psum_t = ctx.enter_context(tc.psum_pool(name="psum_t", bufs=4))
+        psum_o = ctx.enter_context(tc.psum_pool(name="psum_o", bufs=4))
+        if PINNED:
+            ctx.enter_context(tc.manual_schedule())
+
+        ident = keep.tile([P, P], F32, name="ident")
+        make_identity(nc, ident[:])
+
+        x1_of = {}
+        x2_raw = {}
+        for kind, a, n in LOADS:
+            if kind == "x1":
+                tl = keep.tile([P, n * UNIT * K], BF16, name="x1_%d" % a)
+                t0 = (a % UNITS_HEAD) * UNIT
+                nc.sync.dma_start(
+                    out=tl[:].rearrange("p (t k) -> p t k", k=K),
+                    in_=x1h[a // UNITS_HEAD][:, t0:t0 + n * UNIT, :],
+                )
+                for i in range(n):
+                    x1_of[a + i] = (tl, i * UNIT)
+            else:
+                raw = keep.tile([P, 4 * N], BF16, name="x2raw_%d" % a)
+                nc.sync.dma_start(out=raw[:].rearrange("p (u f) -> p u f", u=2), in_=x2h[a])
+                x2_raw[a] = raw
+
+        out_of = {}
+        for a, n in STORES:
+            ot = keep.tile([P, n * UNIT * N], F32, name="out_%d" % a)
+            for i in range(n):
+                out_of[a + i] = (ot, i * UNIT)
+
+        x2_grouped = {}
+        x2_codes = {}
+        x2_scales = {}
+        xt_of = {}
+        grouped_of = {}
+        codes_of = {}
+        scales_of = {}
+        acc_of = {}
+
+        def x2_regroup(h):
+            g2 = keep.tile([P, 4 * N], BF16, name="x2g_%d" % h, align_bytes=64)
+            nc.vector.tensor_copy(
+                out=g2[:].rearrange("p (c i t) -> p c t i", i=4, t=4),
+                in_=x2_raw[h][:].rearrange("p (t c i) -> p c t i", t=4, i=4),
+            )
+            x2_grouped[h] = g2
+
+        def x2_quantise(h):
+            cd = keep.tile([P, N], U32, name="x2c_%d" % h, align_bytes=64)
+            sc = keep.tile([P, N], U8, name="x2s_%d" % h, align_bytes=64)
+            nc.vector.quantize_mx(out=cd[:].bitcast(FP8X4), scales=sc[:], in_=x2_grouped[h][:])
+            x2_codes[h] = cd
+            x2_scales[h] = sc
+
+        def transposes(j):
+            tl, t0 = x1_of[j]
+            words = tl[:].bitcast(F32)
+            banks = []
+            for bnk in range(2):
+                xt = psum_t.tile([P, 512], F32, name="xt", tag="xt")
+                for rt in range(2):
+                    for u in range(2):
+                        col = (t0 + 2 * bnk + rt) * (K // 2) + u * P
+                        slot = (2 * rt + u) * P
+                        nc.tensor.transpose(
+                            out=xt[:, slot:slot + P],
+                            in_=words[:, col:col + P],
+                            identity=ident[:],
+                        )
+                banks.append(xt)
+            xt_of[j] = banks
+
+        def regroup(j):
+            g = gpool.tile([P, UNIT * K], BF16, name="grouped", tag="grouped", align_bytes=64)
+            g32 = g[:].bitcast(F32)
+            for bnk in range(2):
+                dst = g32[:, bnk * 512:(bnk + 1) * 512].rearrange("p (rt r u) -> p rt r u", rt=2, u=2)
+                src = xt_of[j][bnk][:].rearrange("p (rt u r) -> p rt r u", rt=2, u=2)
+                if bnk == 0:
+                    nc.scalar.copy(out=dst, in_=src)
+                else:
+                    nc.vector.tensor_copy(out=dst, in_=src)
+            grouped_of[j] = g
+
+        def quantise(j):
+            cd = cpool.tile([P, UNIT * P], U32, name="codes", tag="codes", align_bytes=64)
+            sc = cpool.tile([P, UNIT * P], U8, name="scales", tag="scales", align_bytes=64)
+            nc.vector.quantize_mx(out=cd[:].bitcast(FP8X4), scales=sc[:], in_=grouped_of[j][:])
+            codes_of[j] = cd
+            scales_of[j] = sc
+
+        def multiply(j):
+            h = j // UNITS_HEAD
+            banks = []
+            for bnk in range(2):
+                acc = psum_o.tile([P, 2 * N], F32, name="acc", tag="acc")
+                for rt in range(2):
+                    c0 = (2 * bnk + rt) * P
+                    nc.tensor.matmul_mx(
+                        out=acc[:, rt * N:(rt + 1) * N],
+                        lhsT=codes_of[j][:, c0:c0 + P].bitcast(FP8X4),
+                        lhsT_scale=scales_of[j][:, c0:c0 + P],
+                        rhs=x2_codes[h][:].bitcast(FP8X4),
+                        rhs_scale=x2_scales[h][:],
+                        start=True,
+                        stop=True,
+                    )
+                banks.append(acc)
+            acc_of[j] = banks
+
+        def copy_out(j):
+            ot, t0 = out_of[j]
+            for bnk in range(2):
+                c0 = (t0 + 2 * bnk) * N
+                if bnk == 1 and j in VEC_OUT:
+                    nc.vector.tensor_copy(out=ot[:, c0:c0 + 2 * N], in_=acc_of[j][bnk][:])
+                else:
+                    nc.scalar.copy(out=ot[:, c0:c0 + 2 * N], in_=acc_of[j][bnk][:])
+
+        def store_after(j):
+            for a, n in STORES:
+                if a + n - 1 == j:
+                    t0 = (a % UNITS_HEAD) * UNIT
+                    nc.sync.dma_start(
+                        out=outh[a // UNITS_HEAD][:, t0:t0 + n * UNIT, :],
+                        in_=out_of[a][0][:].rearrange("p (t n) -> p t n", n=N),
+                    )
+
+        x2_regroup(0)
+        for i in range(NU + 4):
+            if 0 <= i - 3 < NU:
+                multiply(i - 3)
+            if i < NU:
+                transposes(i)
+            if 0 <= i - 1 < NU:
+                regroup(i - 1)
+            if i == 1:
+                x2_quantise(0)
+            if 0 <= i - 2 < NU:
+                quantise(i - 2)
+            if i % UNITS_HEAD == 0 and 0 < i < NU:
+                x2_regroup(i // UNITS_HEAD)
+            if i % UNITS_HEAD == 1 and 1 < i < NU:
+                x2_quantise(i // UNITS_HEAD)
+            if 0 <= i - 4 < NU:
+                copy_out(i - 4)
+                store_after(i - 4)

@@ -24,13 +24,13 @@ FLOPS = 2 * HEADS * ROWS * K * N
 PINNED = True
 
 LOADS = [
-    ("x1", 0, 1), ("x2", 0, 0), ("x1", 1, 1), ("x1", 2, 2),
-    ("x2", 1, 0), ("x1", 4, 2), ("x1", 6, 2),
+    ("x1", 0, 1), ("x2", 0, 0), ("x1", 1, 1), ("x1", 2, 1), ("x1", 3, 1),
+    ("x1", 4, 1), ("x1", 5, 1), ("x2", 1, 0), ("x1", 6, 2),
     ("x2", 2, 0), ("x1", 8, 2), ("x1", 10, 2),
     ("x2", 3, 0), ("x1", 12, 2), ("x1", 14, 2),
 ]
-STORES = [(0, 4), (4, 4), (8, 4), (12, 2), (14, 1), (15, 1)]
-VEC_OUT = (1, 5, 9, 13)
+STORES = [(0, 4), (4, 4), (8, 2), (10, 2), (12, 2), (14, 1), (15, 1)]
+VEC_OUT = (0, 4, 8, 12)
 
 
 def tile_matmul_t_kernel(tc, x1, x2, clip_val1, clip_val2, out):
@@ -122,10 +122,7 @@ def tile_matmul_t_kernel(tc, x1, x2, clip_val1, clip_val2, out):
             for bnk in range(2):
                 dst = g32[:, bnk * 512:(bnk + 1) * 512].rearrange("p (rt r u) -> p rt r u", rt=2, u=2)
                 src = xt_of[j][bnk][:].rearrange("p (rt u r) -> p rt r u", rt=2, u=2)
-                if bnk == 0:
-                    nc.scalar.copy(out=dst, in_=src)
-                else:
-                    nc.vector.tensor_copy(out=dst, in_=src)
+                nc.scalar.copy(out=dst, in_=src)
             grouped_of[j] = g
 
         def quantise(j):
@@ -158,7 +155,7 @@ def tile_matmul_t_kernel(tc, x1, x2, clip_val1, clip_val2, out):
             ot, t0 = out_of[j]
             for bnk in range(2):
                 c0 = (t0 + 2 * bnk) * N
-                if bnk == 1 and j in VEC_OUT:
+                if bnk == 1 or j in VEC_OUT:
                     nc.vector.tensor_copy(out=ot[:, c0:c0 + 2 * N], in_=acc_of[j][bnk][:])
                 else:
                     nc.scalar.copy(out=ot[:, c0:c0 + 2 * N], in_=acc_of[j][bnk][:])
@@ -173,21 +170,20 @@ def tile_matmul_t_kernel(tc, x1, x2, clip_val1, clip_val2, out):
                     )
 
         x2_regroup(0)
-        for i in range(NU + 4):
+        x2_quantise(0)
+        for i in range(NU + 3):
             if 0 <= i - 3 < NU:
                 multiply(i - 3)
             if i < NU:
                 transposes(i)
-            if 0 <= i - 1 < NU:
-                regroup(i - 1)
-            if i == 1:
-                x2_quantise(0)
             if 0 <= i - 2 < NU:
                 quantise(i - 2)
-            if i % UNITS_HEAD == 0 and 0 < i < NU:
-                x2_regroup(i // UNITS_HEAD)
+            if 0 <= i - 1 < NU:
+                regroup(i - 1)
             if i % UNITS_HEAD == 1 and 1 < i < NU:
                 x2_quantise(i // UNITS_HEAD)
-            if 0 <= i - 4 < NU:
-                copy_out(i - 4)
-                store_after(i - 4)
+            if i % UNITS_HEAD == 0 and 0 < i < NU:
+                x2_regroup(i // UNITS_HEAD)
+            if 0 <= i - 3 < NU:
+                copy_out(i - 3)
+                store_after(i - 3)

@@ -24,12 +24,12 @@ FLOPS = 2 * HEADS * ROWS * K * N
 PINNED = True
 
 LOADS = [
-    ("x1", 0, 1), ("x2", 0, 0), ("x1", 1, 1), ("x1", 2, 1), ("x1", 3, 1),
-    ("x1", 4, 1), ("x1", 5, 1), ("x2", 1, 0), ("x1", 6, 2),
+    ("x1", 0, 1), ("x2", 0, 0), ("x1", 1, 1), ("x1", 2, 2),
+    ("x1", 4, 2), ("x2", 1, 0), ("x1", 6, 2),
     ("x2", 2, 0), ("x1", 8, 2), ("x1", 10, 2),
-    ("x2", 3, 0), ("x1", 12, 2), ("x1", 14, 2),
+    ("x2", 3, 0), ("x1", 12, 4),
 ]
-STORES = [(0, 4), (4, 4), (8, 2), (10, 2), (12, 2), (14, 1), (15, 1)]
+STORES = [(0, 4), (4, 4), (8, 2), (10, 2), (12, 2), (14, 2)]
 VEC_OUT = (0, 4, 8, 12)
 
 

@@ -21,7 +21,7 @@ NU = HEADS * UNITS_HEAD
 
 FLOPS = 2 * HEADS * ROWS * K * N
 
-PINNED = True
+PINNED = False
 
 LOADS = [
     ("x1", 0, 1), ("x2", 0, 0), ("x1", 1, 1), ("x1", 2, 2),

from contextlib import ExitStack

import concourse.mybir as mybir
from concourse.masks import make_identity

FP8X4 = mybir.dt.float8_e4m3fn_x4
BF16 = mybir.dt.bfloat16
F32 = mybir.dt.float32
U32 = mybir.dt.uint32
U8 = mybir.dt.uint8

P = 128
HEADS = 4
ROWS = 2048
K = 512
N = 256
T_HEAD = ROWS // P
UNIT = 4
UNITS_HEAD = T_HEAD // UNIT
NU = HEADS * UNITS_HEAD

FLOPS = 2 * HEADS * ROWS * K * N

PINNED = False

LOADS = [
    ("x1", 0, 1), ("x2", 0, 0), ("x1", 1, 1), ("x1", 2, 2),
    ("x1", 4, 2), ("x2", 1, 0), ("x1", 6, 2),
    ("x2", 2, 0), ("x1", 8, 2), ("x1", 10, 2),
    ("x2", 3, 0), ("x1", 12, 4),
]
STORES = [(0, 4), (4, 4), (8, 2), (10, 2), (12, 2), (14, 2)]
VEC_OUT = (0, 4, 8, 12)


def tile_matmul_t_kernel(tc, x1, x2, clip_val1, clip_val2, out):
    nc = tc.nc
    x1h = [x1[b, h].rearrange("(p t) k -> p t k", t=T_HEAD) for b in range(2) for h in range(2)]
    x2h = [x2[b, h].rearrange("(u q e) c -> q u (e c)", u=2, e=2) for b in range(2) for h in range(2)]
    outh = [out[b, h].rearrange("(p t) n -> p t n", t=T_HEAD) for b in range(2) for h in range(2)]

    with ExitStack() as ctx:
        keep = ctx.enter_context(tc.tile_pool(name="keep", bufs=1))
        gpool = ctx.enter_context(tc.tile_pool(name="gpool", bufs=3))
        cpool = ctx.enter_context(tc.tile_pool(name="cpool", bufs=3))
        psum_t = ctx.enter_context(tc.psum_pool(name="psum_t", bufs=4))
        psum_o = ctx.enter_context(tc.psum_pool(name="psum_o", bufs=4))
        if PINNED:
            ctx.enter_context(tc.manual_schedule())

        ident = keep.tile([P, P], F32, name="ident")
        make_identity(nc, ident[:])

        x1_of = {}
        x2_raw = {}
        for kind, a, n in LOADS:
            if kind == "x1":
                tl = keep.tile([P, n * UNIT * K], BF16, name="x1_%d" % a)
                t0 = (a % UNITS_HEAD) * UNIT
                nc.sync.dma_start(
                    out=tl[:].rearrange("p (t k) -> p t k", k=K),
                    in_=x1h[a // UNITS_HEAD][:, t0:t0 + n * UNIT, :],
                )
                for i in range(n):
                    x1_of[a + i] = (tl, i * UNIT)
            else:
                raw = keep.tile([P, 4 * N], BF16, name="x2raw_%d" % a)
                nc.sync.dma_start(out=raw[:].rearrange("p (u f) -> p u f", u=2), in_=x2h[a])
                x2_raw[a] = raw

        out_of = {}
        for a, n in STORES:
            ot = keep.tile([P, n * UNIT * N], F32, name="out_%d" % a)
            for i in range(n):
                out_of[a + i] = (ot, i * UNIT)

        x2_grouped = {}
        x2_codes = {}
        x2_scales = {}
        xt_of = {}
        grouped_of = {}
        codes_of = {}
        scales_of = {}
        acc_of = {}

        def x2_regroup(h):
            g2 = keep.tile([P, 4 * N], BF16, name="x2g_%d" % h, align_bytes=64)
            nc.vector.tensor_copy(
                out=g2[:].rearrange("p (c i t) -> p c t i", i=4, t=4),
                in_=x2_raw[h][:].rearrange("p (t c i) -> p c t i", t=4, i=4),
            )
            x2_grouped[h] = g2

        def x2_quantise(h):
            cd = keep.tile([P, N], U32, name="x2c_%d" % h, align_bytes=64)
            sc = keep.tile([P, N], U8, name="x2s_%d" % h, align_bytes=64)
            nc.vector.quantize_mx(out=cd[:].bitcast(FP8X4), scales=sc[:], in_=x2_grouped[h][:])
            x2_codes[h] = cd
            x2_scales[h] = sc

        def transposes(j):
            tl, t0 = x1_of[j]
            words = tl[:].bitcast(F32)
            banks = []
            for bnk in range(2):
                xt = psum_t.tile([P, 512], F32, name="xt", tag="xt")
                for rt in range(2):
                    for u in range(2):
                        col = (t0 + 2 * bnk + rt) * (K // 2) + u * P
                        slot = (2 * rt + u) * P
                        nc.tensor.transpose(
                            out=xt[:, slot:slot + P],
                            in_=words[:, col:col + P],
                            identity=ident[:],
                        )
                banks.append(xt)
            xt_of[j] = banks

        def regroup(j):
            g = gpool.tile([P, UNIT * K], BF16, name="grouped", tag="grouped", align_bytes=64)
            g32 = g[:].bitcast(F32)
            for bnk in range(2):
                dst = g32[:, bnk * 512:(bnk + 1) * 512].rearrange("p (rt r u) -> p rt r u", rt=2, u=2)
                src = xt_of[j][bnk][:].rearrange("p (rt u r) -> p rt r u", rt=2, u=2)
                nc.scalar.copy(out=dst, in_=src)
            grouped_of[j] = g

        def quantise(j):
            cd = cpool.tile([P, UNIT * P], U32, name="codes", tag="codes", align_bytes=64)
            sc = cpool.tile([P, UNIT * P], U8, name="scales", tag="scales", align_bytes=64)
            nc.vector.quantize_mx(out=cd[:].bitcast(FP8X4), scales=sc[:], in_=grouped_of[j][:])
            codes_of[j] = cd
            scales_of[j] = sc

        def multiply(j):
            h = j // UNITS_HEAD
            banks = []
            for bnk in range(2):
                acc = psum_o.tile([P, 2 * N], F32, name="acc", tag="acc")
                for rt in range(2):
                    c0 = (2 * bnk + rt) * P
                    nc.tensor.matmul_mx(
                        out=acc[:, rt * N:(rt + 1) * N],
                        lhsT=codes_of[j][:, c0:c0 + P].bitcast(FP8X4),
                        lhsT_scale=scales_of[j][:, c0:c0 + P],
                        rhs=x2_codes[h][:].bitcast(FP8X4),
                        rhs_scale=x2_scales[h][:],
                        start=True,
                        stop=True,
                    )
                banks.append(acc)
            acc_of[j] = banks

        def copy_out(j):
            ot, t0 = out_of[j]
            for bnk in range(2):
                c0 = (t0 + 2 * bnk) * N
                if bnk == 1 or j in VEC_OUT:
                    nc.vector.tensor_copy(out=ot[:, c0:c0 + 2 * N], in_=acc_of[j][bnk][:])
                else:
                    nc.scalar.copy(out=ot[:, c0:c0 + 2 * N], in_=acc_of[j][bnk][:])

        def store_after(j):
            for a, n in STORES:
                if a + n - 1 == j:
                    t0 = (a % UNITS_HEAD) * UNIT
                    nc.sync.dma_start(
                        out=outh[a // UNITS_HEAD][:, t0:t0 + n * UNIT, :],
                        in_=out_of[a][0][:].rearrange("p (t n) -> p t n", n=N),
                    )

        x2_regroup(0)
        x2_quantise(0)
        for i in range(NU + 3):
            if 0 <= i - 3 < NU:
                multiply(i - 3)
            if i < NU:
                transposes(i)
            if 0 <= i - 2 < NU:
                quantise(i - 2)
            if 0 <= i - 1 < NU:
                regroup(i - 1)
            if i % UNITS_HEAD == 1 and 1 < i < NU:
                x2_quantise(i // UNITS_HEAD)
            if i % UNITS_HEAD == 0 and 0 < i < NU:
                x2_regroup(i // UNITS_HEAD)
            if 0 <= i - 3 < NU:
                copy_out(i - 3)
                store_after(i - 3)
